import numpy as np
import ml_dtypes


def mxq(x, axis, fmt="e4m3"):
    dtype, down = {"e4m3": (ml_dtypes.float8_e4m3fn, 7), "e5m2": (ml_dtypes.float8_e5m2, 14)}[fmt]
    v = np.moveaxis(np.asarray(x, np.float32).astype(ml_dtypes.bfloat16).astype(np.float64), axis, -1)
    blocks = v.reshape(v.shape[:-1] + (-1, 32))
    amax = np.abs(blocks).max(-1, keepdims=True)
    byte = np.maximum(np.where(amax > 0, np.frexp(amax)[1] - 1 + 127, 0) - down, 1)
    scale = np.exp2(byte - 127.0)
    codes = (blocks / scale).astype(np.float32).astype(dtype).astype(np.float64)
    return np.moveaxis((codes * scale).reshape(v.shape), -1, axis)


WIDE = False


def mx_kscale(k):
    if not WIDE:
        return np.ones(k)
    levels = np.array([10, -10, 5, -5, 0])
    a = np.random.permutation(np.resize(levels, k // 512 * 4)).reshape(k // 512, 4)
    idx = np.arange(k)
    return np.exp2(a[idx // 512, idx % 128 // 32])


BF16 = ml_dtypes.bfloat16


def bf(x):
    return np.asarray(x, np.float32).astype(BF16)


def f64(x):
    return np.asarray(x).astype(np.float64)


E, D_NODE, D_EDGE, D_GLOB, LATENT, D_OUT = 16384, 128, 128, 128, 128, 128
D_IN = D_NODE + D_NODE + D_EDGE + D_GLOB


def setup_inputs():
    s = mx_kscale(D_IN)
    o1 = D_NODE
    o2 = o1 + D_NODE
    o3 = o2 + D_EDGE
    return {
        "receiver": bf(np.random.standard_normal((E, D_NODE)) * s[:o1]),
        "sender": bf(np.random.standard_normal((E, D_NODE)) * s[o1:o2]),
        "edge_attr": bf(np.random.standard_normal((E, D_EDGE)) * s[o2:o3]),
        "global_attr": bf(np.random.standard_normal((1, D_GLOB)) * s[o3:]),
        "W1": bf(np.random.standard_normal((D_IN, LATENT)) / np.sqrt(D_IN) / s[:, None]),
        "b1": bf(np.random.standard_normal(LATENT) * 0.1),
    }


def reference(receiver, sender, edge_attr, global_attr, W1, b1):
    e = edge_attr.shape[0]
    g = np.tile(f64(global_attr), (e // global_attr.shape[0], 1))
    x = np.concatenate([f64(receiver), f64(sender), f64(edge_attr), g], axis=1)
    return np.maximum((mxq(x, 1, "e4m3") @ mxq(f64(W1), 0, "e4m3")) + f64(b1), 0.0)

@@ -1,0 +1,242 @@
+from contextlib import ExitStack
+
+import concourse.mybir as mybir
+from concourse.masks import make_identity
+
+F32 = mybir.dt.float32
+BF16 = mybir.dt.bfloat16
+U32 = mybir.dt.uint32
+U8 = mybir.dt.uint8
+I32 = mybir.dt.int32
+FP8X4 = mybir.dt.float8_e4m3fn_x4
+ADD = mybir.AluOpType.add
+MAX = mybir.AluOpType.max
+RELU = mybir.ActivationFunctionType.Relu
+
+P = 128
+E = 16384
+D = 128
+NG = 16
+LOAD_CHUNKS = (1, 1, 2, 4, 4, 4)
+
+FLOPS = 2 * E * 512 * D
+
+
+def tile_edgemodel_pa_t_kernel(tc, receiver, sender, edge_attr, global_attr, W1, b1, out):
+    nc = tc.nc
+    with ExitStack() as ctx:
+        const = ctx.enter_context(tc.tile_pool(name="const", bufs=1))
+        work = ctx.enter_context(tc.tile_pool(name="work", bufs=3))
+        pt = ctx.enter_context(tc.psum_pool(name="pt", bufs=2))
+        po = ctx.enter_context(tc.psum_pool(name="po", bufs=2))
+        ctx.enter_context(tc.manual_schedule())
+
+        xr = const.tile([P, E], BF16, name="xr")
+        xs = const.tile([P, E], BF16, name="xs")
+        xe = const.tile([P, E], BF16, name="xe")
+        osb = const.tile([P, E], F32, name="osb")
+        streams = ((xr, receiver), (xs, sender), (xe, edge_attr))
+        out_v = out.rearrange("(p t) n -> p (t n)", p=P)
+
+        ident = const.tile([P, P], F32, name="ident")
+        make_identity(nc, ident[:])
+
+        wt1raw = const.tile([P, 4, D], BF16, name="wt1raw")
+        wt2raw = const.tile([P, 4, D], BF16, name="wt2raw")
+        wgraw = const.tile([P, 4, D], BF16, name="wgraw")
+        g4 = const.tile([P, 4], BF16, name="g4")
+        bb = const.tile([P, D], BF16, name="bb")
+        wt1in = const.tile([P, 1024], BF16, name="wt1in", align_bytes=64)
+        wt2in = const.tile([P, 2048], BF16, name="wt2in", align_bytes=64)
+        wgin = const.tile([P, 512], BF16, name="wgin", align_bytes=64)
+        gin = const.tile([P, 512], BF16, name="gin", align_bytes=64)
+        wt1c = const.tile([P, 256], U32, name="wt1c", align_bytes=64)
+        wt2c = const.tile([P, 512], U32, name="wt2c", align_bytes=64)
+        wgc = const.tile([P, 128], U32, name="wgc", align_bytes=64)
+        gc = const.tile([P, 128], U32, name="gc", align_bytes=64)
+        wt1s = const.tile([P, 256], U8, name="wt1s", align_bytes=64)
+        wt2s = const.tile([P, 512], U8, name="wt2s", align_bytes=64)
+        wgs = const.tile([P, 128], U8, name="wgs", align_bytes=64)
+        gs = const.tile([P, 128], U8, name="gs", align_bytes=64)
+        bt1 = const.tile([P, D], F32, name="bt1")
+        bias = const.tile([P, 4, D], F32, name="bias")
+
+        for z in (wt1in, wt2in, gin, wgin):
+            nc.vector.memset(z[:].bitcast(I32), 0)
+
+        w_edge = W1[256:384, :].rearrange("(i t) n -> i t n", t=4)
+        for j in range(4):
+            nc.scalar.dma_start(out=wt2raw[32 * j : 32 * j + 32, :, :], in_=w_edge)
+        w_rs = W1[0:256, :].rearrange("(u q e) n -> q u (e n)", u=2, q=64, e=2)
+        for h in range(2):
+            nc.gpsimd.dma_start(
+                out=wt1raw[64 * h : 64 * h + 64, :, :].rearrange("q (u e) n -> q u (e n)", u=2, e=2),
+                in_=w_rs,
+            )
+        first = 0
+        for ci, n_groups in enumerate(LOAD_CHUNKS):
+            cols = slice(1024 * first, 1024 * (first + n_groups))
+            for x_sb, x_dram in streams:
+                nc.sync.dma_start(out=x_sb[:, cols], in_=x_dram.rearrange("(p t) f -> p (t f)", p=P)[:, cols])
+            first += n_groups
+            if ci == 0:
+                nc.scalar.dma_start(out=bb[:], in_=b1.partition_broadcast(P))
+                nc.scalar.dma_start(out=g4[0:32, :], in_=global_attr.rearrange("o (i t) -> (o i) t", t=4))
+                nc.scalar.dma_start(
+                    out=wgraw[0:32, :, :], in_=W1[384:512, :].rearrange("(i t) n -> i t n", t=4)
+                )
+
+        state = {}
+
+        def transposes(g):
+            banks = []
+            for s in range(2):
+                t1 = pt.tile([P, 2, 256], F32, name="t1_%d" % s, tag="t1_%d" % s)
+                for u, x_sb in ((0, xr), (1, xs)):
+                    words = x_sb[:].bitcast(F32)
+                    for h in range(2):
+                        w0 = 512 * g + 256 * s + 128 * h
+                        nc.tensor.transpose(t1[:, u, 128 * h : 128 * h + 128], words[:, w0 : w0 + 128], ident[:])
+                banks.append(t1)
+            t2 = pt.tile([P, 2, 256], F32, name="t2", tag="t2")
+            words = xe[:].bitcast(F32)
+            for s in range(2):
+                w0 = 512 * g + 256 * s
+                pairs = words[:, w0 : w0 + 256].rearrange("p (m u) -> p m u", u=2)
+                for u in range(2):
+                    nc.tensor.transpose(t2[:, u, 128 * s : 128 * s + 128], pairs[:, :, u], ident[:])
+            banks.append(t2)
+            state[("banks", g)] = banks
+
+        def evacuate(g):
+            grouped = work.tile([P, 3, 1024], BF16, name="grouped", tag="grouped", align_bytes=64)
+            for b, bank in enumerate(state[("banks", g)]):
+                nc.scalar.copy(
+                    out=grouped[:, b, :].bitcast(F32).rearrange("p (c u) -> p c u", u=2),
+                    in_=bank[:].rearrange("p u c -> p c u"),
+                )
+            state[("grouped", g)] = grouped
+
+        def quantise(g):
+            codes = work.tile([P, 3, 256], U32, name="codes", tag="codes", align_bytes=64)
+            scales = work.tile([P, 3, 256], U8, name="scales", tag="scales", align_bytes=64)
+            grouped = state[("grouped", g)]
+            for b in range(3):
+                nc.vector.quantize_mx(
+                    out=codes[:, b, :].bitcast(FP8X4), scales=scales[:, b, :], in_=grouped[:, b, :]
+                )
+            state[("codes", g)] = (codes, scales)
+
+        def multiply(g, s):
+            codes, scales = state[("codes", g)]
+            o = po.tile([P, 512], F32, name="o", tag="o")
+            for h in range(2):
+                cols = slice(256 * h, 256 * h + 256)
+                e_cols = slice(128 * s, 128 * s + 128)
+                nc.tensor.matmul_mx(
+                    out=o[:, cols],
+                    lhsT=codes[:, 2, e_cols].bitcast(FP8X4),
+                    lhsT_scale=scales[:, 2, e_cols],
+                    rhs=wt2c[:, cols].bitcast(FP8X4),
+                    rhs_scale=wt2s[:, cols],
+                    start=True,
+                    stop=False,
+                )
+                rs_cols = slice(128 * h, 128 * h + 128)
+                nc.tensor.matmul_mx(
+                    out=o[:, cols],
+                    lhsT=codes[:, s, rs_cols].bitcast(FP8X4),
+                    lhsT_scale=scales[:, s, rs_cols],
+                    rhs=wt1c[:].bitcast(FP8X4),
+                    rhs_scale=wt1s[:],
+                    start=False,
+                    stop=True,
+                )
+            state[("o", g, s)] = o
+
+        def out_cols(g, s):
+            return slice(1024 * g + 512 * s, 1024 * g + 512 * s + 512)
+
+        def add_bias(g, s):
+            nc.vector.tensor_tensor(
+                out=osb[:, out_cols(g, s)],
+                in0=state[("o", g, s)][:],
+                in1=bias[:].rearrange("p j n -> p (j n)"),
+                op=ADD,
+            )
+
+        def relu_gpsimd(g, s):
+            nc.gpsimd.tensor_scalar(
+                out=osb[:, out_cols(g, s)], in0=osb[:, out_cols(g, s)], scalar1=0.0, scalar2=0.0, op0=MAX, op1=ADD
+            )
+
+        def relu_scalar(g, s):
+            nc.scalar.activation(out=osb[:, out_cols(g, s)], in_=osb[:, out_cols(g, s)], func=RELU)
+
+        def store(cols):
+            nc.sync.dma_start(out=out_v[:, cols], in_=osb[:, cols])
+
+        transposes(0)
+        wt2v = wt2in[:].rearrange("p (c t) -> p c t", t=4)
+        for j in range(4):
+            rows = slice(32 * j, 32 * j + 32)
+            nc.scalar.copy(
+                out=wt2v[rows, 128 * j : 128 * j + 128, :], in_=wt2raw[rows, :, :].rearrange("p t n -> p n t")
+            )
+        wt1v = wt1in[:].rearrange("p (c t) -> p c t", t=4)
+        for h in range(2):
+            rows = slice(64 * h, 64 * h + 64)
+            nc.vector.tensor_copy(
+                out=wt1v[rows, 128 * h : 128 * h + 128, :], in_=wt1raw[rows, :, :].rearrange("p t n -> p n t")
+            )
+        nc.vector.tensor_copy(
+            out=gin[:].rearrange("p (c t) -> p c t", t=4)[0:32, :, :],
+            in_=g4[0:32, :].unsqueeze(1).to_broadcast([32, 128, 4]),
+        )
+        nc.vector.tensor_copy(
+            out=wgin[:].rearrange("p (c t) -> p c t", t=4)[0:32, :, :],
+            in_=wgraw[0:32, :, :].rearrange("p t n -> p n t"),
+        )
+        nc.vector.quantize_mx(out=wt1c[:].bitcast(FP8X4), scales=wt1s[:], in_=wt1in[:])
+        nc.vector.quantize_mx(out=gc[:].bitcast(FP8X4), scales=gs[:], in_=gin[:])
+        nc.vector.quantize_mx(out=wgc[:].bitcast(FP8X4), scales=wgs[:], in_=wgin[:])
+        nc.vector.quantize_mx(out=wt2c[:].bitcast(FP8X4), scales=wt2s[:], in_=wt2in[:])
+        evacuate(0)
+        transposes(1)
+        evacuate(1)
+        quantise(0)
+        cps = po.tile([P, 512], F32, name="cps", tag="o")
+        nc.tensor.matmul_mx(
+            out=cps[:, 0:128],
+            lhsT=gc[:].bitcast(FP8X4),
+            lhsT_scale=gs[:],
+            rhs=wgc[:].bitcast(FP8X4),
+            rhs_scale=wgs[:],
+            start=True,
+            stop=True,
+        )
+        multiply(0, 0)
+        nc.vector.tensor_tensor(out=bt1[:], in0=cps[:, 0:128], in1=bb[:], op=ADD)
+        nc.vector.tensor_copy(out=bias[:], in_=bt1[:].unsqueeze(1).to_broadcast([P, 4, D]))
+        multiply(0, 1)
+
+        for g in range(NG):
+            if g + 2 < NG:
+                transposes(g + 2)
+            if g >= 1:
+                relu_scalar(g - 1, 1)
+                store(slice(1024 * (g - 1), 1024 * g))
+            if g + 2 < NG:
+                evacuate(g + 2)
+            if g + 1 < NG:
+                quantise(g + 1)
+            add_bias(g, 0)
+            relu_gpsimd(g, 0)
+            if g + 1 < NG:
+                multiply(g + 1, 0)
+            add_bias(g, 1)
+            if g + 1 < NG:
+                multiply(g + 1, 1)
+        store(out_cols(NG - 1, 0))
+        relu_scalar(NG - 1, 1)
+        store(out_cols(NG - 1, 1))

@@ -10,7 +10,6 @@ U8 = mybir.dt.uint8
 I32 = mybir.dt.int32
 FP8X4 = mybir.dt.float8_e4m3fn_x4
 ADD = mybir.AluOpType.add
-MAX = mybir.AluOpType.max
 RELU = mybir.ActivationFunctionType.Relu
 
 P = 128
@@ -165,10 +164,8 @@ def tile_edgemodel_pa_t_kernel(tc, receiver, sender, edge_attr, global_attr, W1,
                 op=ADD,
             )
 
-        def relu_gpsimd(g, s):
-            nc.gpsimd.tensor_scalar(
-                out=osb[:, out_cols(g, s)], in0=osb[:, out_cols(g, s)], scalar1=0.0, scalar2=0.0, op0=MAX, op1=ADD
-            )
+        def relu_vector(g, s):
+            nc.vector.tensor_scalar_max(out=osb[:, out_cols(g, s)], in0=osb[:, out_cols(g, s)], scalar1=0.0)
 
         def relu_scalar(g, s):
             nc.scalar.activation(out=osb[:, out_cols(g, s)], in_=osb[:, out_cols(g, s)], func=RELU)
@@ -231,12 +228,12 @@ def tile_edgemodel_pa_t_kernel(tc, receiver, sender, edge_attr, global_attr, W1,
             if g + 1 < NG:
                 quantise(g + 1)
             add_bias(g, 0)
-            relu_gpsimd(g, 0)
             if g + 1 < NG:
                 multiply(g + 1, 0)
             add_bias(g, 1)
             if g + 1 < NG:
                 multiply(g + 1, 1)
+            relu_vector(g, 0)
         store(out_cols(NG - 1, 0))
         relu_scalar(NG - 1, 1)
         store(out_cols(NG - 1, 1))

@@ -16,7 +16,7 @@ P = 128
 E = 16384
 D = 128
 NG = 16
-LOAD_CHUNKS = (1, 1, 2, 4, 4, 4)
+LOAD_CHUNKS = (1, 1, 1, 1, 2, 2, 4, 4)
 
 FLOPS = 2 * E * 512 * D
 
@@ -153,22 +153,24 @@ def tile_edgemodel_pa_t_kernel(tc, receiver, sender, edge_attr, global_attr, W1,
                 )
             state[("o", g, s)] = o
 
-        def out_cols(g, s):
-            return slice(1024 * g + 512 * s, 1024 * g + 512 * s + 512)
+        def out_cols(g, s, lo=0, hi=512):
+            return slice(1024 * g + 512 * s + lo, 1024 * g + 512 * s + hi)
 
-        def add_bias(g, s):
+        def add_bias(g, s, lo=0, hi=512):
             nc.vector.tensor_tensor(
-                out=osb[:, out_cols(g, s)],
-                in0=state[("o", g, s)][:],
-                in1=bias[:].rearrange("p j n -> p (j n)"),
+                out=osb[:, out_cols(g, s, lo, hi)],
+                in0=state[("o", g, s)][:, lo:hi],
+                in1=bias[:].rearrange("p j n -> p (j n)")[:, lo:hi],
                 op=ADD,
             )
 
-        def relu_vector(g, s):
-            nc.vector.tensor_scalar_max(out=osb[:, out_cols(g, s)], in0=osb[:, out_cols(g, s)], scalar1=0.0)
+        def relu_vector(g, s, lo=0, hi=512):
+            cols = out_cols(g, s, lo, hi)
+            nc.vector.tensor_scalar_max(out=osb[:, cols], in0=osb[:, cols], scalar1=0.0)
 
-        def relu_scalar(g, s):
-            nc.scalar.activation(out=osb[:, out_cols(g, s)], in_=osb[:, out_cols(g, s)], func=RELU)
+        def relu_scalar(g, s, lo=0, hi=512):
+            cols = out_cols(g, s, lo, hi)
+            nc.scalar.activation(out=osb[:, cols], in_=osb[:, cols], func=RELU)
 
         def store(cols):
             nc.sync.dma_start(out=out_v[:, cols], in_=osb[:, cols])
@@ -217,7 +219,7 @@ def tile_edgemodel_pa_t_kernel(tc, receiver, sender, edge_attr, global_attr, W1,
         nc.vector.tensor_copy(out=bias[:], in_=bt1[:].unsqueeze(1).to_broadcast([P, 4, D]))
         multiply(0, 1)
 
-        for g in range(NG):
+        for g in range(NG - 1):
             if g + 2 < NG:
                 transposes(g + 2)
             if g >= 1:
@@ -234,6 +236,14 @@ def tile_edgemodel_pa_t_kernel(tc, receiver, sender, edge_attr, global_attr, W1,
             if g + 1 < NG:
                 multiply(g + 1, 1)
             relu_vector(g, 0)
-        store(out_cols(NG - 1, 0))
-        relu_scalar(NG - 1, 1)
-        store(out_cols(NG - 1, 1))
+        last = NG - 1
+        relu_scalar(last - 1, 1)
+        store(slice(1024 * (last - 1), 1024 * last))
+        add_bias(last, 0)
+        relu_scalar(last, 0)
+        store(out_cols(last, 0))
+        add_bias(last, 1)
+        relu_scalar(last, 1, 0, 256)
+        relu_vector(last, 1, 256, 512)
+        store(out_cols(last, 1, 256, 512))
+        store(out_cols(last, 1, 0, 256))

@@ -18,6 +18,8 @@ D = 128
 NG = 16
 LOAD_CHUNKS = (1, 1, 1, 1, 2, 2, 4, 4)
 
+V_RELU = 256
+
 FLOPS = 2 * E * 512 * D
 
 
@@ -223,7 +225,7 @@ def tile_edgemodel_pa_t_kernel(tc, receiver, sender, edge_attr, global_attr, W1,
             if g + 2 < NG:
                 transposes(g + 2)
             if g >= 1:
-                relu_scalar(g - 1, 1)
+                relu_scalar(g - 1, 0, V_RELU, 1024)
                 store(slice(1024 * (g - 1), 1024 * g))
             if g + 2 < NG:
                 evacuate(g + 2)
@@ -235,9 +237,9 @@ def tile_edgemodel_pa_t_kernel(tc, receiver, sender, edge_attr, global_attr, W1,
             add_bias(g, 1)
             if g + 1 < NG:
                 multiply(g + 1, 1)
-            relu_vector(g, 0)
+            relu_vector(g, 0, 0, V_RELU)
         last = NG - 1
-        relu_scalar(last - 1, 1)
+        relu_scalar(last - 1, 0, V_RELU, 1024)
         store(slice(1024 * (last - 1), 1024 * last))
         add_bias(last, 0)
         relu_scalar(last, 0)

@@ -18,8 +18,6 @@ D = 128
 NG = 16
 LOAD_CHUNKS = (1, 1, 1, 1, 2, 2, 4, 4)
 
-V_RELU = 256
-
 FLOPS = 2 * E * 512 * D
 
 
@@ -220,26 +218,27 @@ def tile_edgemodel_pa_t_kernel(tc, receiver, sender, edge_attr, global_attr, W1,
         nc.vector.tensor_tensor(out=bt1[:], in0=cps[:, 0:128], in1=bb[:], op=ADD)
         nc.vector.tensor_copy(out=bias[:], in_=bt1[:].unsqueeze(1).to_broadcast([P, 4, D]))
         multiply(0, 1)
+        transposes(2)
+        evacuate(2)
+        quantise(1)
 
-        for g in range(NG - 1):
+        for g in range(1, NG):
             if g + 2 < NG:
                 transposes(g + 2)
-            if g >= 1:
-                relu_scalar(g - 1, 0, V_RELU, 1024)
-                store(slice(1024 * (g - 1), 1024 * g))
+            if g >= 2:
+                relu_scalar(g - 2, 1)
+                store(slice(1024 * (g - 2), 1024 * (g - 1)))
             if g + 2 < NG:
                 evacuate(g + 2)
+            add_bias(g - 1, 0)
+            multiply(g, 0)
+            add_bias(g - 1, 1)
+            multiply(g, 1)
             if g + 1 < NG:
                 quantise(g + 1)
-            add_bias(g, 0)
-            if g + 1 < NG:
-                multiply(g + 1, 0)
-            add_bias(g, 1)
-            if g + 1 < NG:
-                multiply(g + 1, 1)
-            relu_vector(g, 0, 0, V_RELU)
+            relu_vector(g - 1, 0)
         last = NG - 1
-        relu_scalar(last - 1, 0, V_RELU, 1024)
+        relu_scalar(last - 1, 1)
         store(slice(1024 * (last - 1), 1024 * last))
         add_bias(last, 0)
         relu_scalar(last, 0)

@@ -40,13 +40,14 @@ def tile_edgemodel_pa_t_kernel(tc, receiver, sender, edge_attr, global_attr, W1,
         ident = const.tile([P, P], F32, name="ident")
         make_identity(nc, ident[:])
 
-        wt1raw = const.tile([P, 4, D], BF16, name="wt1raw")
-        wt2raw = const.tile([P, 4, D], BF16, name="wt2raw")
+        wraw = const.tile([P, 2, 4, D], BF16, name="wraw")
+        win = const.tile([P, 2, D, 4], BF16, name="win", align_bytes=64)
+        wq = const.tile([P, 2, D], U32, name="wq", align_bytes=64)
+        wqs = const.tile([P, 2, D], U8, name="wqs", align_bytes=64)
         wgraw = const.tile([P, 4, D], BF16, name="wgraw")
         g4 = const.tile([P, 4], BF16, name="g4")
-        bb = const.tile([P, D], BF16, name="bb")
-        wt1in = const.tile([P, 1024], BF16, name="wt1in", align_bytes=64)
-        wt2in = const.tile([P, 2048], BF16, name="wt2in", align_bytes=64)
+        brow = const.tile([P, D], BF16, name="brow")
+        ones = const.tile([P, P], BF16, name="ones")
         wgin = const.tile([P, 512], BF16, name="wgin", align_bytes=64)
         gin = const.tile([P, 512], BF16, name="gin", align_bytes=64)
         wt1c = const.tile([P, 256], U32, name="wt1c", align_bytes=64)
@@ -57,33 +58,35 @@ def tile_edgemodel_pa_t_kernel(tc, receiver, sender, edge_attr, global_attr, W1,
         wt2s = const.tile([P, 512], U8, name="wt2s", align_bytes=64)
         wgs = const.tile([P, 128], U8, name="wgs", align_bytes=64)
         gs = const.tile([P, 128], U8, name="gs", align_bytes=64)
-        bt1 = const.tile([P, D], F32, name="bt1")
-        bias = const.tile([P, 4, D], F32, name="bias")
+        bsb = const.tile([P, D], F32, name="bsb")
+        bias = const.tile([P, D], F32, name="bias")
 
-        for z in (wt1in, wt2in, gin, wgin):
-            nc.vector.memset(z[:].bitcast(I32), 0)
+        nc.vector.memset(brow[:].bitcast(I32), 0)
+        nc.vector.memset(ones[:], 1.0)
+        for z in (wqs, wt1c, wt2c, gin, wgin):
+            flat = z[:] if len(z.shape) == 2 else z[:].rearrange("p w n -> p (w n)")
+            nc.vector.memset(flat.bitcast(I32), 0)
 
         w_edge = W1[256:384, :].rearrange("(i t) n -> i t n", t=4)
         for j in range(4):
-            nc.scalar.dma_start(out=wt2raw[32 * j : 32 * j + 32, :, :], in_=w_edge)
+            queue = nc.sync if j < 2 else nc.scalar
+            queue.dma_start(out=wraw[32 * j : 32 * j + 32, 0, :, :], in_=w_edge)
         w_rs = W1[0:256, :].rearrange("(u q e) n -> q u (e n)", u=2, q=64, e=2)
         for h in range(2):
-            nc.gpsimd.dma_start(
-                out=wt1raw[64 * h : 64 * h + 64, :, :].rearrange("q (u e) n -> q u (e n)", u=2, e=2),
+            nc.scalar.dma_start(
+                out=wraw[64 * h : 64 * h + 64, 1, :, :].rearrange("q (u e) n -> q u (e n)", u=2, e=2),
                 in_=w_rs,
             )
         first = 0
-        for ci, n_groups in enumerate(LOAD_CHUNKS):
+        for n_groups in LOAD_CHUNKS:
             cols = slice(1024 * first, 1024 * (first + n_groups))
             for x_sb, x_dram in streams:
                 nc.sync.dma_start(out=x_sb[:, cols], in_=x_dram.rearrange("(p t) f -> p (t f)", p=P)[:, cols])
+            if first == 0:
+                nc.sync.dma_start(out=wgraw[0:32, :, :], in_=W1[384:512, :].rearrange("(i t) n -> i t n", t=4))
+                nc.sync.dma_start(out=g4[0:32, :], in_=global_attr.rearrange("o (i t) -> (o i) t", t=4))
+                nc.sync.dma_start(out=brow[0:1, :], in_=b1.unsqueeze(0))
             first += n_groups
-            if ci == 0:
-                nc.scalar.dma_start(out=bb[:], in_=b1.partition_broadcast(P))
-                nc.scalar.dma_start(out=g4[0:32, :], in_=global_attr.rearrange("o (i t) -> (o i) t", t=4))
-                nc.scalar.dma_start(
-                    out=wgraw[0:32, :, :], in_=W1[384:512, :].rearrange("(i t) n -> i t n", t=4)
-                )
 
         state = {}
 
@@ -157,10 +160,11 @@ def tile_edgemodel_pa_t_kernel(tc, receiver, sender, edge_attr, global_attr, W1,
             return slice(1024 * g + 512 * s + lo, 1024 * g + 512 * s + hi)
 
         def add_bias(g, s, lo=0, hi=512):
+            n_edges = (hi - lo) // D
             nc.vector.tensor_tensor(
-                out=osb[:, out_cols(g, s, lo, hi)],
-                in0=state[("o", g, s)][:, lo:hi],
-                in1=bias[:].rearrange("p j n -> p (j n)")[:, lo:hi],
+                out=osb[:, out_cols(g, s, lo, hi)].rearrange("p (j n) -> p j n", n=D),
+                in0=state[("o", g, s)][:, lo:hi].rearrange("p (j n) -> p j n", n=D),
+                in1=bias[:].unsqueeze(1).to_broadcast([P, n_edges, D]),
                 op=ADD,
             )
 
@@ -176,18 +180,30 @@ def tile_edgemodel_pa_t_kernel(tc, receiver, sender, edge_attr, global_attr, W1,
             nc.sync.dma_start(out=out_v[:, cols], in_=osb[:, cols])
 
         transposes(0)
-        wt2v = wt2in[:].rearrange("p (c t) -> p c t", t=4)
+        nc.scalar.copy(out=win[:, 0, :, :], in_=wraw[:, 0, :, :].rearrange("p t n -> p n t"))
+        evacuate(0)
+        nc.vector.tensor_copy(out=win[:, 1, :, :], in_=wraw[:, 1, :, :].rearrange("p t n -> p n t"))
+        nc.vector.quantize_mx(
+            out=wq[:].rearrange("p w n -> p (w n)").bitcast(FP8X4),
+            scales=wqs[:].rearrange("p w n -> p (w n)"),
+            in_=win[:].rearrange("p w n t -> p (w n t)"),
+        )
+        codes_i = wq[:].bitcast(I32)
+        scales_i = wqs[:].bitcast(I32)
         for j in range(4):
             rows = slice(32 * j, 32 * j + 32)
-            nc.scalar.copy(
-                out=wt2v[rows, 128 * j : 128 * j + 128, :], in_=wt2raw[rows, :, :].rearrange("p t n -> p n t")
-            )
-        wt1v = wt1in[:].rearrange("p (c t) -> p c t", t=4)
+            nc.vector.tensor_copy(out=wt2c[rows, 128 * j : 128 * j + 128].bitcast(I32), in_=codes_i[rows, 0, :])
+            nc.vector.tensor_copy(out=wt2s[:, 128 * j : 128 * j + 128].bitcast(I32), in_=scales_i[:, 0, :])
         for h in range(2):
             rows = slice(64 * h, 64 * h + 64)
-            nc.vector.tensor_copy(
-                out=wt1v[rows, 128 * h : 128 * h + 128, :], in_=wt1raw[rows, :, :].rearrange("p t n -> p n t")
-            )
+            nc.vector.tensor_copy(out=wt1c[rows, 128 * h : 128 * h + 128].bitcast(I32), in_=codes_i[rows, 1, :])
+            nc.vector.tensor_copy(out=wt1s[:, 128 * h : 128 * h + 128].bitcast(I32), in_=scales_i[:, 1, :])
+        transposes(1)
+        cps = po.tile([P, 512], F32, name="cps", tag="o")
+        nc.tensor.matmul(out=cps[:, 128:256], lhsT=ones[:], rhs=brow[:], start=True, stop=True)
+        evacuate(1)
+        nc.scalar.copy(out=bsb[:], in_=cps[:, 128:256])
+        quantise(0)
         nc.vector.tensor_copy(
             out=gin[:].rearrange("p (c t) -> p c t", t=4)[0:32, :, :],
             in_=g4[0:32, :].unsqueeze(1).to_broadcast([32, 128, 4]),
@@ -196,15 +212,8 @@ def tile_edgemodel_pa_t_kernel(tc, receiver, sender, edge_attr, global_attr, W1,
             out=wgin[:].rearrange("p (c t) -> p c t", t=4)[0:32, :, :],
             in_=wgraw[0:32, :, :].rearrange("p t n -> p n t"),
         )
-        nc.vector.quantize_mx(out=wt1c[:].bitcast(FP8X4), scales=wt1s[:], in_=wt1in[:])
         nc.vector.quantize_mx(out=gc[:].bitcast(FP8X4), scales=gs[:], in_=gin[:])
         nc.vector.quantize_mx(out=wgc[:].bitcast(FP8X4), scales=wgs[:], in_=wgin[:])
-        nc.vector.quantize_mx(out=wt2c[:].bitcast(FP8X4), scales=wt2s[:], in_=wt2in[:])
-        evacuate(0)
-        transposes(1)
-        evacuate(1)
-        quantise(0)
-        cps = po.tile([P, 512], F32, name="cps", tag="o")
         nc.tensor.matmul_mx(
             out=cps[:, 0:128],
             lhsT=gc[:].bitcast(FP8X4),
@@ -215,8 +224,7 @@ def tile_edgemodel_pa_t_kernel(tc, receiver, sender, edge_attr, global_attr, W1,
             stop=True,
         )
         multiply(0, 0)
-        nc.vector.tensor_tensor(out=bt1[:], in0=cps[:, 0:128], in1=bb[:], op=ADD)
-        nc.vector.tensor_copy(out=bias[:], in_=bt1[:].unsqueeze(1).to_broadcast([P, 4, D]))
+        nc.vector.tensor_tensor(out=bias[:], in0=cps[:, 0:128], in1=bsb[:], op=ADD)
         multiply(0, 1)
         transposes(2)
         evacuate(2)

@@ -123,36 +123,37 @@ def tile_edgemodel_pa_t_kernel(tc, receiver, sender, edge_attr, global_attr, W1,
             codes = work.tile([P, 3, 256], U32, name="codes", tag="codes", align_bytes=64)
             scales = work.tile([P, 3, 256], U8, name="scales", tag="scales", align_bytes=64)
             grouped = state[("grouped", g)]
-            for b in range(3):
+            for b0, b1_ in ((0, 2), (2, 3)):
                 nc.vector.quantize_mx(
-                    out=codes[:, b, :].bitcast(FP8X4), scales=scales[:, b, :], in_=grouped[:, b, :]
+                    out=codes[:, b0:b1_, :].rearrange("p b c -> p (b c)").bitcast(FP8X4),
+                    scales=scales[:, b0:b1_, :].rearrange("p b c -> p (b c)"),
+                    in_=grouped[:, b0:b1_, :].rearrange("p b c -> p (b c)"),
                 )
             state[("codes", g)] = (codes, scales)
 
         def multiply(g, s):
             codes, scales = state[("codes", g)]
             o = po.tile([P, 512], F32, name="o", tag="o")
+            e_cols = slice(128 * s, 128 * s + 128)
+            nc.tensor.matmul_mx(
+                out=o[:],
+                lhsT=codes[:, 2, e_cols].bitcast(FP8X4),
+                lhsT_scale=scales[:, 2, e_cols],
+                rhs=wt2c[:].bitcast(FP8X4),
+                rhs_scale=wt2s[:],
+                start=True,
+                stop=False,
+            )
             for h in range(2):
-                cols = slice(256 * h, 256 * h + 256)
-                e_cols = slice(128 * s, 128 * s + 128)
-                nc.tensor.matmul_mx(
-                    out=o[:, cols],
-                    lhsT=codes[:, 2, e_cols].bitcast(FP8X4),
-                    lhsT_scale=scales[:, 2, e_cols],
-                    rhs=wt2c[:, cols].bitcast(FP8X4),
-                    rhs_scale=wt2s[:, cols],
-                    start=True,
-                    stop=False,
-                )
                 rs_cols = slice(128 * h, 128 * h + 128)
                 nc.tensor.matmul_mx(
-                    out=o[:, cols],
+                    out=o[:, 256 * h : 256 * h + 256],
                     lhsT=codes[:, s, rs_cols].bitcast(FP8X4),
                     lhsT_scale=scales[:, s, rs_cols],
                     rhs=wt1c[:].bitcast(FP8X4),
                     rhs_scale=wt1s[:],
                     start=False,
-                    stop=True,
+                    stop=h == 1,
                 )
             state[("o", g, s)] = o
 
@@ -193,11 +194,14 @@ def tile_edgemodel_pa_t_kernel(tc, receiver, sender, edge_attr, global_attr, W1,
         for j in range(4):
             rows = slice(32 * j, 32 * j + 32)
             nc.vector.tensor_copy(out=wt2c[rows, 128 * j : 128 * j + 128].bitcast(I32), in_=codes_i[rows, 0, :])
-            nc.vector.tensor_copy(out=wt2s[:, 128 * j : 128 * j + 128].bitcast(I32), in_=scales_i[:, 0, :])
         for h in range(2):
             rows = slice(64 * h, 64 * h + 64)
             nc.vector.tensor_copy(out=wt1c[rows, 128 * h : 128 * h + 128].bitcast(I32), in_=codes_i[rows, 1, :])
-            nc.vector.tensor_copy(out=wt1s[:, 128 * h : 128 * h + 128].bitcast(I32), in_=scales_i[:, 1, :])
+        for slot, n_blocks, planes in ((0, 4, wt2s), (1, 2, wt1s)):
+            nc.vector.tensor_copy(
+                out=planes[:].bitcast(I32).rearrange("p (j c) -> p j c", j=n_blocks),
+                in_=scales_i[:, slot, :].unsqueeze(1).to_broadcast([P, n_blocks, D // 4]),
+            )
         transposes(1)
         cps = po.tile([P, 512], F32, name="cps", tag="o")
         nc.tensor.matmul(out=cps[:, 128:256], lhsT=ones[:], rhs=brow[:], start=True, stop=True)

@@ -15,6 +15,7 @@ RELU = mybir.ActivationFunctionType.Relu
 P = 128
 E = 16384
 D = 128
+V_RELU = 384
 NG = 16
 LOAD_CHUNKS = (1, 1, 1, 1, 2, 2, 4, 4)
 
@@ -203,6 +204,7 @@ def tile_edgemodel_pa_t_kernel(tc, receiver, sender, edge_attr, global_attr, W1,
                 in_=scales_i[:, slot, :].unsqueeze(1).to_broadcast([P, n_blocks, D // 4]),
             )
         transposes(1)
+        transposes(2)
         cps = po.tile([P, 512], F32, name="cps", tag="o")
         nc.tensor.matmul(out=cps[:, 128:256], lhsT=ones[:], rhs=brow[:], start=True, stop=True)
         evacuate(1)
@@ -228,17 +230,16 @@ def tile_edgemodel_pa_t_kernel(tc, receiver, sender, edge_attr, global_attr, W1,
             stop=True,
         )
         multiply(0, 0)
+        quantise(1)
         nc.vector.tensor_tensor(out=bias[:], in0=cps[:, 0:128], in1=bsb[:], op=ADD)
         multiply(0, 1)
-        transposes(2)
         evacuate(2)
-        quantise(1)
 
         for g in range(1, NG):
             if g + 2 < NG:
                 transposes(g + 2)
             if g >= 2:
-                relu_scalar(g - 2, 1)
+                relu_scalar(g - 2, 0, V_RELU, 1024)
                 store(slice(1024 * (g - 2), 1024 * (g - 1)))
             if g + 2 < NG:
                 evacuate(g + 2)
@@ -248,15 +249,15 @@ def tile_edgemodel_pa_t_kernel(tc, receiver, sender, edge_attr, global_attr, W1,
             multiply(g, 1)
             if g + 1 < NG:
                 quantise(g + 1)
-            relu_vector(g - 1, 0)
+            if g + 1 < NG:
+                relu_vector(g - 1, 0, 0, V_RELU)
         last = NG - 1
-        relu_scalar(last - 1, 1)
-        store(slice(1024 * (last - 1), 1024 * last))
+        for s in range(2):
+            relu_scalar(last - 1, s)
+            store(out_cols(last - 1, s))
         add_bias(last, 0)
         relu_scalar(last, 0)
         store(out_cols(last, 0))
         add_bias(last, 1)
-        relu_scalar(last, 1, 0, 256)
-        relu_vector(last, 1, 256, 512)
-        store(out_cols(last, 1, 256, 512))
-        store(out_cols(last, 1, 0, 256))
+        relu_vector(last, 1)
+        store(out_cols(last, 1))

@@ -17,7 +17,7 @@ E = 16384
 D = 128
 V_RELU = 384
 NG = 16
-LOAD_CHUNKS = (1, 1, 1, 1, 2, 2, 4, 4)
+LOAD_CHUNKS = (1, 1, 1, 2, 3, 4, 4)
 
 FLOPS = 2 * E * 512 * D
 
@@ -41,11 +41,12 @@ def tile_edgemodel_pa_t_kernel(tc, receiver, sender, edge_attr, global_attr, W1,
         ident = const.tile([P, P], F32, name="ident")
         make_identity(nc, ident[:])
 
-        wraw = const.tile([P, 2, 4, D], BF16, name="wraw")
+        wn = const.tile([P, 4, D], BF16, name="wn")
+        spread = const.tile([P, P], BF16, name="spread")
+        wrs = const.tile([P, 4, D], BF16, name="wrs")
         win = const.tile([P, 2, D, 4], BF16, name="win", align_bytes=64)
         wq = const.tile([P, 2, D], U32, name="wq", align_bytes=64)
         wqs = const.tile([P, 2, D], U8, name="wqs", align_bytes=64)
-        wgraw = const.tile([P, 4, D], BF16, name="wgraw")
         g4 = const.tile([P, 4], BF16, name="g4")
         brow = const.tile([P, D], BF16, name="brow")
         ones = const.tile([P, P], BF16, name="ones")
@@ -68,25 +69,19 @@ def tile_edgemodel_pa_t_kernel(tc, receiver, sender, edge_attr, global_attr, W1,
             flat = z[:] if len(z.shape) == 2 else z[:].rearrange("p w n -> p (w n)")
             nc.vector.memset(flat.bitcast(I32), 0)
 
-        w_edge = W1[256:384, :].rearrange("(i t) n -> i t n", t=4)
-        for j in range(4):
-            queue = nc.sync if j < 2 else nc.scalar
-            queue.dma_start(out=wraw[32 * j : 32 * j + 32, 0, :, :], in_=w_edge)
+        nc.scalar.dma_start(out=wn[:], in_=W1.rearrange("(i t) n -> i t n", t=4))
         w_rs = W1[0:256, :].rearrange("(u q e) n -> q u (e n)", u=2, q=64, e=2)
         for h in range(2):
             nc.scalar.dma_start(
-                out=wraw[64 * h : 64 * h + 64, 1, :, :].rearrange("q (u e) n -> q u (e n)", u=2, e=2),
-                in_=w_rs,
+                out=wrs[64 * h : 64 * h + 64, :, :].rearrange("q (u e) n -> q u (e n)", u=2, e=2), in_=w_rs
             )
+        nc.gpsimd.dma_start(out=g4[96:128, :], in_=global_attr.rearrange("o (i t) -> (o i) t", t=4))
+        nc.gpsimd.dma_start(out=brow[0:1, :], in_=b1.unsqueeze(0))
         first = 0
         for n_groups in LOAD_CHUNKS:
             cols = slice(1024 * first, 1024 * (first + n_groups))
             for x_sb, x_dram in streams:
                 nc.sync.dma_start(out=x_sb[:, cols], in_=x_dram.rearrange("(p t) f -> p (t f)", p=P)[:, cols])
-            if first == 0:
-                nc.sync.dma_start(out=wgraw[0:32, :, :], in_=W1[384:512, :].rearrange("(i t) n -> i t n", t=4))
-                nc.sync.dma_start(out=g4[0:32, :], in_=global_attr.rearrange("o (i t) -> (o i) t", t=4))
-                nc.sync.dma_start(out=brow[0:1, :], in_=b1.unsqueeze(0))
             first += n_groups
 
         state = {}
@@ -181,10 +176,18 @@ def tile_edgemodel_pa_t_kernel(tc, receiver, sender, edge_attr, global_attr, W1,
         def store(cols):
             nc.sync.dma_start(out=out_v[:, cols], in_=osb[:, cols])
 
+        nc.vector.tensor_copy(
+            out=spread[:].rearrange("p (j i) -> p j i", j=4),
+            in_=ident[:, 64:96].unsqueeze(1).to_broadcast([P, 4, 32]),
+        )
+        wps = po.tile([P, 512], F32, name="wps", tag="o")
+        nc.tensor.matmul(
+            out=wps[:], lhsT=spread[:], rhs=wn[:].rearrange("p t n -> p (t n)"), start=True, stop=True
+        )
+        nc.scalar.copy(out=win[:, 0, :, :], in_=wps[:].rearrange("p (t n) -> p n t", t=4))
         transposes(0)
-        nc.scalar.copy(out=win[:, 0, :, :], in_=wraw[:, 0, :, :].rearrange("p t n -> p n t"))
         evacuate(0)
-        nc.vector.tensor_copy(out=win[:, 1, :, :], in_=wraw[:, 1, :, :].rearrange("p t n -> p n t"))
+        nc.vector.tensor_copy(out=win[:, 1, :, :], in_=wrs[:].rearrange("p t n -> p n t"))
         nc.vector.quantize_mx(
             out=wq[:].rearrange("p w n -> p (w n)").bitcast(FP8X4),
             scales=wqs[:].rearrange("p w n -> p (w n)"),
@@ -211,12 +214,12 @@ def tile_edgemodel_pa_t_kernel(tc, receiver, sender, edge_attr, global_attr, W1,
         nc.scalar.copy(out=bsb[:], in_=cps[:, 128:256])
         quantise(0)
         nc.vector.tensor_copy(
-            out=gin[:].rearrange("p (c t) -> p c t", t=4)[0:32, :, :],
-            in_=g4[0:32, :].unsqueeze(1).to_broadcast([32, 128, 4]),
+            out=gin[:].rearrange("p (c t) -> p c t", t=4)[96:128, :, :],
+            in_=g4[96:128, :].unsqueeze(1).to_broadcast([32, 128, 4]),
         )
         nc.vector.tensor_copy(
-            out=wgin[:].rearrange("p (c t) -> p c t", t=4)[0:32, :, :],
-            in_=wgraw[0:32, :, :].rearrange("p t n -> p n t"),
+            out=wgin[:].rearrange("p (c t) -> p c t", t=4)[96:128, :, :],
+            in_=wn[96:128, :, :].rearrange("p t n -> p n t"),
         )
         nc.vector.quantize_mx(out=gc[:].bitcast(FP8X4), scales=gs[:], in_=gin[:])
         nc.vector.quantize_mx(out=wgc[:].bitcast(FP8X4), scales=wgs[:], in_=wgin[:])
@@ -240,7 +243,10 @@ def tile_edgemodel_pa_t_kernel(tc, receiver, sender, edge_attr, global_attr, W1,
                 transposes(g + 2)
             if g >= 2:
                 relu_scalar(g - 2, 0, V_RELU, 1024)
-                store(slice(1024 * (g - 2), 1024 * (g - 1)))
+                if g - 2 >= 10:
+                    store(slice(1024 * (g - 2), 1024 * (g - 1)))
+                elif g % 2 == 1:
+                    store(slice(1024 * (g - 3), 1024 * (g - 1)))
             if g + 2 < NG:
                 evacuate(g + 2)
             add_bias(g - 1, 0)

@@ -1,7 +1,6 @@
 from contextlib import ExitStack
 
 import concourse.mybir as mybir
-from concourse.masks import make_identity
 
 F32 = mybir.dt.float32
 BF16 = mybir.dt.bfloat16
@@ -10,12 +9,13 @@ U8 = mybir.dt.uint8
 I32 = mybir.dt.int32
 FP8X4 = mybir.dt.float8_e4m3fn_x4
 ADD = mybir.AluOpType.add
+NOT_EQUAL = mybir.AluOpType.not_equal
 RELU = mybir.ActivationFunctionType.Relu
 
 P = 128
 E = 16384
 D = 128
-V_RELU = 384
+V_RELU = 512
 NG = 16
 LOAD_CHUNKS = (1, 1, 1, 2, 3, 4, 4)
 
@@ -28,21 +28,40 @@ def tile_edgemodel_pa_t_kernel(tc, receiver, sender, edge_attr, global_attr, W1,
         const = ctx.enter_context(tc.tile_pool(name="const", bufs=1))
         work = ctx.enter_context(tc.tile_pool(name="work", bufs=3))
         pt = ctx.enter_context(tc.psum_pool(name="pt", bufs=2))
-        po = ctx.enter_context(tc.psum_pool(name="po", bufs=2))
+        po = ctx.enter_context(tc.psum_pool(name="po", bufs=3))
         ctx.enter_context(tc.manual_schedule())
 
         xr = const.tile([P, E], BF16, name="xr")
         xs = const.tile([P, E], BF16, name="xs")
         xe = const.tile([P, E], BF16, name="xe")
         osb = const.tile([P, E], F32, name="osb")
-        streams = ((xr, receiver), (xs, sender), (xe, edge_attr))
+        streams = ((xe, edge_attr), (xr, receiver), (xs, sender))
         out_v = out.rearrange("(p t) n -> p (t n)", p=P)
 
         ident = const.tile([P, P], F32, name="ident")
-        make_identity(nc, ident[:])
+        spread = const.tile([P, P], BF16, name="spread")
+        nc.vector.memset(ident[:], 0.0)
+        nc.vector.memset(spread[:], 0.0)
+        nc.gpsimd.affine_select(
+            out=ident[:],
+            in_=ident[:],
+            compare_op=NOT_EQUAL,
+            fill=1.0,
+            base=0,
+            pattern=[[-1, P]],
+            channel_multiplier=1,
+        )
+        nc.gpsimd.affine_select(
+            out=spread[:],
+            in_=spread[:],
+            compare_op=NOT_EQUAL,
+            fill=1.0,
+            base=-64,
+            pattern=[[0, 4], [-1, 32]],
+            channel_multiplier=1,
+        )
 
         wn = const.tile([P, 4, D], BF16, name="wn")
-        spread = const.tile([P, P], BF16, name="spread")
         wrs = const.tile([P, 4, D], BF16, name="wrs")
         win = const.tile([P, 2, D, 4], BF16, name="win", align_bytes=64)
         wq = const.tile([P, 2, D], U32, name="wq", align_bytes=64)
@@ -75,19 +94,27 @@ def tile_edgemodel_pa_t_kernel(tc, receiver, sender, edge_attr, global_attr, W1,
             nc.scalar.dma_start(
                 out=wrs[64 * h : 64 * h + 64, :, :].rearrange("q (u e) n -> q u (e n)", u=2, e=2), in_=w_rs
             )
-        nc.gpsimd.dma_start(out=g4[96:128, :], in_=global_attr.rearrange("o (i t) -> (o i) t", t=4))
-        nc.gpsimd.dma_start(out=brow[0:1, :], in_=b1.unsqueeze(0))
         first = 0
         for n_groups in LOAD_CHUNKS:
             cols = slice(1024 * first, 1024 * (first + n_groups))
             for x_sb, x_dram in streams:
                 nc.sync.dma_start(out=x_sb[:, cols], in_=x_dram.rearrange("(p t) f -> p (t f)", p=P)[:, cols])
+            if first == 0:
+                nc.sync.dma_start(out=g4[96:128, :], in_=global_attr.rearrange("o (i t) -> (o i) t", t=4))
+                nc.sync.dma_start(out=brow[0:1, :], in_=b1.unsqueeze(0))
             first += n_groups
 
         state = {}
 
         def transposes(g):
-            banks = []
+            t2 = pt.tile([P, 2, 256], F32, name="t2", tag="t2", bufs=1)
+            words = xe[:].bitcast(F32)
+            for s in range(2):
+                w0 = 512 * g + 256 * s
+                pairs = words[:, w0 : w0 + 256].rearrange("p (m u) -> p m u", u=2)
+                for u in range(2):
+                    nc.tensor.transpose(t2[:, u, 128 * s : 128 * s + 128], pairs[:, :, u], ident[:])
+            banks = [t2]
             for s in range(2):
                 t1 = pt.tile([P, 2, 256], F32, name="t1_%d" % s, tag="t1_%d" % s)
                 for u, x_sb in ((0, xr), (1, xs)):
@@ -96,14 +123,6 @@ def tile_edgemodel_pa_t_kernel(tc, receiver, sender, edge_attr, global_attr, W1,
                         w0 = 512 * g + 256 * s + 128 * h
                         nc.tensor.transpose(t1[:, u, 128 * h : 128 * h + 128], words[:, w0 : w0 + 128], ident[:])
                 banks.append(t1)
-            t2 = pt.tile([P, 2, 256], F32, name="t2", tag="t2")
-            words = xe[:].bitcast(F32)
-            for s in range(2):
-                w0 = 512 * g + 256 * s
-                pairs = words[:, w0 : w0 + 256].rearrange("p (m u) -> p m u", u=2)
-                for u in range(2):
-                    nc.tensor.transpose(t2[:, u, 128 * s : 128 * s + 128], pairs[:, :, u], ident[:])
-            banks.append(t2)
             state[("banks", g)] = banks
 
         def evacuate(g):
@@ -119,7 +138,7 @@ def tile_edgemodel_pa_t_kernel(tc, receiver, sender, edge_attr, global_attr, W1,
             codes = work.tile([P, 3, 256], U32, name="codes", tag="codes", align_bytes=64)
             scales = work.tile([P, 3, 256], U8, name="scales", tag="scales", align_bytes=64)
             grouped = state[("grouped", g)]
-            for b0, b1_ in ((0, 2), (2, 3)):
+            for b0, b1_ in ((0, 1), (1, 3)):
                 nc.vector.quantize_mx(
                     out=codes[:, b0:b1_, :].rearrange("p b c -> p (b c)").bitcast(FP8X4),
                     scales=scales[:, b0:b1_, :].rearrange("p b c -> p (b c)"),
@@ -133,8 +152,8 @@ def tile_edgemodel_pa_t_kernel(tc, receiver, sender, edge_attr, global_attr, W1,
             e_cols = slice(128 * s, 128 * s + 128)
             nc.tensor.matmul_mx(
                 out=o[:],
-                lhsT=codes[:, 2, e_cols].bitcast(FP8X4),
-                lhsT_scale=scales[:, 2, e_cols],
+                lhsT=codes[:, 0, e_cols].bitcast(FP8X4),
+                lhsT_scale=scales[:, 0, e_cols],
                 rhs=wt2c[:].bitcast(FP8X4),
                 rhs_scale=wt2s[:],
                 start=True,
@@ -144,8 +163,8 @@ def tile_edgemodel_pa_t_kernel(tc, receiver, sender, edge_attr, global_attr, W1,
                 rs_cols = slice(128 * h, 128 * h + 128)
                 nc.tensor.matmul_mx(
                     out=o[:, 256 * h : 256 * h + 256],
-                    lhsT=codes[:, s, rs_cols].bitcast(FP8X4),
-                    lhsT_scale=scales[:, s, rs_cols],
+                    lhsT=codes[:, 1 + s, rs_cols].bitcast(FP8X4),
+                    lhsT_scale=scales[:, 1 + s, rs_cols],
                     rhs=wt1c[:].bitcast(FP8X4),
                     rhs_scale=wt1s[:],
                     start=False,
@@ -176,10 +195,6 @@ def tile_edgemodel_pa_t_kernel(tc, receiver, sender, edge_attr, global_attr, W1,
         def store(cols):
             nc.sync.dma_start(out=out_v[:, cols], in_=osb[:, cols])
 
-        nc.vector.tensor_copy(
-            out=spread[:].rearrange("p (j i) -> p j i", j=4),
-            in_=ident[:, 64:96].unsqueeze(1).to_broadcast([P, 4, 32]),
-        )
         wps = po.tile([P, 512], F32, name="wps", tag="o")
         nc.tensor.matmul(
             out=wps[:], lhsT=spread[:], rhs=wn[:].rearrange("p t n -> p (t n)"), start=True, stop=True

from contextlib import ExitStack

import concourse.mybir as mybir

F32 = mybir.dt.float32
BF16 = mybir.dt.bfloat16
U32 = mybir.dt.uint32
U8 = mybir.dt.uint8
I32 = mybir.dt.int32
FP8X4 = mybir.dt.float8_e4m3fn_x4
ADD = mybir.AluOpType.add
NOT_EQUAL = mybir.AluOpType.not_equal
RELU = mybir.ActivationFunctionType.Relu

P = 128
E = 16384
D = 128
V_RELU = 512
NG = 16
LOAD_CHUNKS = (1, 1, 1, 2, 3, 4, 4)

FLOPS = 2 * E * 512 * D


def tile_edgemodel_pa_t_kernel(tc, receiver, sender, edge_attr, global_attr, W1, b1, out):
    nc = tc.nc
    with ExitStack() as ctx:
        const = ctx.enter_context(tc.tile_pool(name="const", bufs=1))
        work = ctx.enter_context(tc.tile_pool(name="work", bufs=3))
        pt = ctx.enter_context(tc.psum_pool(name="pt", bufs=2))
        po = ctx.enter_context(tc.psum_pool(name="po", bufs=3))
        ctx.enter_context(tc.manual_schedule())

        xr = const.tile([P, E], BF16, name="xr")
        xs = const.tile([P, E], BF16, name="xs")
        xe = const.tile([P, E], BF16, name="xe")
        osb = const.tile([P, E], F32, name="osb")
        streams = ((xe, edge_attr), (xr, receiver), (xs, sender))
        out_v = out.rearrange("(p t) n -> p (t n)", p=P)

        ident = const.tile([P, P], F32, name="ident")
        spread = const.tile([P, P], BF16, name="spread")
        nc.vector.memset(ident[:], 0.0)
        nc.vector.memset(spread[:], 0.0)
        nc.gpsimd.affine_select(
            out=ident[:],
            in_=ident[:],
            compare_op=NOT_EQUAL,
            fill=1.0,
            base=0,
            pattern=[[-1, P]],
            channel_multiplier=1,
        )
        nc.gpsimd.affine_select(
            out=spread[:],
            in_=spread[:],
            compare_op=NOT_EQUAL,
            fill=1.0,
            base=-64,
            pattern=[[0, 4], [-1, 32]],
            channel_multiplier=1,
        )

        wn = const.tile([P, 4, D], BF16, name="wn")
        wrs = const.tile([P, 4, D], BF16, name="wrs")
        win = const.tile([P, 2, D, 4], BF16, name="win", align_bytes=64)
        wq = const.tile([P, 2, D], U32, name="wq", align_bytes=64)
        wqs = const.tile([P, 2, D], U8, name="wqs", align_bytes=64)
        g4 = const.tile([P, 4], BF16, name="g4")
        brow = const.tile([P, D], BF16, name="brow")
        ones = const.tile([P, P], BF16, name="ones")
        wgin = const.tile([P, 512], BF16, name="wgin", align_bytes=64)
        gin = const.tile([P, 512], BF16, name="gin", align_bytes=64)
        wt1c = const.tile([P, 256], U32, name="wt1c", align_bytes=64)
        wt2c = const.tile([P, 512], U32, name="wt2c", align_bytes=64)
        wgc = const.tile([P, 128], U32, name="wgc", align_bytes=64)
        gc = const.tile([P, 128], U32, name="gc", align_bytes=64)
        wt1s = const.tile([P, 256], U8, name="wt1s", align_bytes=64)
        wt2s = const.tile([P, 512], U8, name="wt2s", align_bytes=64)
        wgs = const.tile([P, 128], U8, name="wgs", align_bytes=64)
        gs = const.tile([P, 128], U8, name="gs", align_bytes=64)
        bsb = const.tile([P, D], F32, name="bsb")
        bias = const.tile([P, D], F32, name="bias")

        nc.vector.memset(brow[:].bitcast(I32), 0)
        nc.vector.memset(ones[:], 1.0)
        for z in (wqs, wt1c, wt2c, gin, wgin):
            flat = z[:] if len(z.shape) == 2 else z[:].rearrange("p w n -> p (w n)")
            nc.vector.memset(flat.bitcast(I32), 0)

        nc.scalar.dma_start(out=wn[:], in_=W1.rearrange("(i t) n -> i t n", t=4))
        w_rs = W1[0:256, :].rearrange("(u q e) n -> q u (e n)", u=2, q=64, e=2)
        for h in range(2):
            nc.scalar.dma_start(
                out=wrs[64 * h : 64 * h + 64, :, :].rearrange("q (u e) n -> q u (e n)", u=2, e=2), in_=w_rs
            )
        first = 0
        for n_groups in LOAD_CHUNKS:
            cols = slice(1024 * first, 1024 * (first + n_groups))
            for x_sb, x_dram in streams:
                nc.sync.dma_start(out=x_sb[:, cols], in_=x_dram.rearrange("(p t) f -> p (t f)", p=P)[:, cols])
            if first == 0:
                nc.sync.dma_start(out=g4[96:128, :], in_=global_attr.rearrange("o (i t) -> (o i) t", t=4))
                nc.sync.dma_start(out=brow[0:1, :], in_=b1.unsqueeze(0))
            first += n_groups

        state = {}

        def transposes(g):
            t2 = pt.tile([P, 2, 256], F32, name="t2", tag="t2", bufs=1)
            words = xe[:].bitcast(F32)
            for s in range(2):
                w0 = 512 * g + 256 * s
                pairs = words[:, w0 : w0 + 256].rearrange("p (m u) -> p m u", u=2)
                for u in range(2):
                    nc.tensor.transpose(t2[:, u, 128 * s : 128 * s + 128], pairs[:, :, u], ident[:])
            banks = [t2]
            for s in range(2):
                t1 = pt.tile([P, 2, 256], F32, name="t1_%d" % s, tag="t1_%d" % s)
                for u, x_sb in ((0, xr), (1, xs)):
                    words = x_sb[:].bitcast(F32)
                    for h in range(2):
                        w0 = 512 * g + 256 * s + 128 * h
                        nc.tensor.transpose(t1[:, u, 128 * h : 128 * h + 128], words[:, w0 : w0 + 128], ident[:])
                banks.append(t1)
            state[("banks", g)] = banks

        def evacuate(g):
            grouped = work.tile([P, 3, 1024], BF16, name="grouped", tag="grouped", align_bytes=64)
            for b, bank in enumerate(state[("banks", g)]):
                nc.scalar.copy(
                    out=grouped[:, b, :].bitcast(F32).rearrange("p (c u) -> p c u", u=2),
                    in_=bank[:].rearrange("p u c -> p c u"),
                )
            state[("grouped", g)] = grouped

        def quantise(g):
            codes = work.tile([P, 3, 256], U32, name="codes", tag="codes", align_bytes=64)
            scales = work.tile([P, 3, 256], U8, name="scales", tag="scales", align_bytes=64)
            grouped = state[("grouped", g)]
            for b0, b1_ in ((0, 1), (1, 3)):
                nc.vector.quantize_mx(
                    out=codes[:, b0:b1_, :].rearrange("p b c -> p (b c)").bitcast(FP8X4),
                    scales=scales[:, b0:b1_, :].rearrange("p b c -> p (b c)"),
                    in_=grouped[:, b0:b1_, :].rearrange("p b c -> p (b c)"),
                )
            state[("codes", g)] = (codes, scales)

        def multiply(g, s):
            codes, scales = state[("codes", g)]
            o = po.tile([P, 512], F32, name="o", tag="o")
            e_cols = slice(128 * s, 128 * s + 128)
            nc.tensor.matmul_mx(
                out=o[:],
                lhsT=codes[:, 0, e_cols].bitcast(FP8X4),
                lhsT_scale=scales[:, 0, e_cols],
                rhs=wt2c[:].bitcast(FP8X4),
                rhs_scale=wt2s[:],
                start=True,
                stop=False,
            )
            for h in range(2):
                rs_cols = slice(128 * h, 128 * h + 128)
                nc.tensor.matmul_mx(
                    out=o[:, 256 * h : 256 * h + 256],
                    lhsT=codes[:, 1 + s, rs_cols].bitcast(FP8X4),
                    lhsT_scale=scales[:, 1 + s, rs_cols],
                    rhs=wt1c[:].bitcast(FP8X4),
                    rhs_scale=wt1s[:],
                    start=False,
                    stop=h == 1,
                )
            state[("o", g, s)] = o

        def out_cols(g, s, lo=0, hi=512):
            return slice(1024 * g + 512 * s + lo, 1024 * g + 512 * s + hi)

        def add_bias(g, s, lo=0, hi=512):
            n_edges = (hi - lo) // D
            nc.vector.tensor_tensor(
                out=osb[:, out_cols(g, s, lo, hi)].rearrange("p (j n) -> p j n", n=D),
                in0=state[("o", g, s)][:, lo:hi].rearrange("p (j n) -> p j n", n=D),
                in1=bias[:].unsqueeze(1).to_broadcast([P, n_edges, D]),
                op=ADD,
            )

        def relu_vector(g, s, lo=0, hi=512):
            cols = out_cols(g, s, lo, hi)
            nc.vector.tensor_scalar_max(out=osb[:, cols], in0=osb[:, cols], scalar1=0.0)

        def relu_scalar(g, s, lo=0, hi=512):
            cols = out_cols(g, s, lo, hi)
            nc.scalar.activation(out=osb[:, cols], in_=osb[:, cols], func=RELU)

        def store(cols):
            nc.sync.dma_start(out=out_v[:, cols], in_=osb[:, cols])

        wps = po.tile([P, 512], F32, name="wps", tag="o")
        nc.tensor.matmul(
            out=wps[:], lhsT=spread[:], rhs=wn[:].rearrange("p t n -> p (t n)"), start=True, stop=True
        )
        nc.scalar.copy(out=win[:, 0, :, :], in_=wps[:].rearrange("p (t n) -> p n t", t=4))
        transposes(0)
        evacuate(0)
        nc.vector.tensor_copy(out=win[:, 1, :, :], in_=wrs[:].rearrange("p t n -> p n t"))
        nc.vector.quantize_mx(
            out=wq[:].rearrange("p w n -> p (w n)").bitcast(FP8X4),
            scales=wqs[:].rearrange("p w n -> p (w n)"),
            in_=win[:].rearrange("p w n t -> p (w n t)"),
        )
        codes_i = wq[:].bitcast(I32)
        scales_i = wqs[:].bitcast(I32)
        for j in range(4):
            rows = slice(32 * j, 32 * j + 32)
            nc.vector.tensor_copy(out=wt2c[rows, 128 * j : 128 * j + 128].bitcast(I32), in_=codes_i[rows, 0, :])
        for h in range(2):
            rows = slice(64 * h, 64 * h + 64)
            nc.vector.tensor_copy(out=wt1c[rows, 128 * h : 128 * h + 128].bitcast(I32), in_=codes_i[rows, 1, :])
        for slot, n_blocks, planes in ((0, 4, wt2s), (1, 2, wt1s)):
            nc.vector.tensor_copy(
                out=planes[:].bitcast(I32).rearrange("p (j c) -> p j c", j=n_blocks),
                in_=scales_i[:, slot, :].unsqueeze(1).to_broadcast([P, n_blocks, D // 4]),
            )
        transposes(1)
        transposes(2)
        cps = po.tile([P, 512], F32, name="cps", tag="o")
        nc.tensor.matmul(out=cps[:, 128:256], lhsT=ones[:], rhs=brow[:], start=True, stop=True)
        evacuate(1)
        nc.scalar.copy(out=bsb[:], in_=cps[:, 128:256])
        quantise(0)
        nc.vector.tensor_copy(
            out=gin[:].rearrange("p (c t) -> p c t", t=4)[96:128, :, :],
            in_=g4[96:128, :].unsqueeze(1).to_broadcast([32, 128, 4]),
        )
        nc.vector.tensor_copy(
            out=wgin[:].rearrange("p (c t) -> p c t", t=4)[96:128, :, :],
            in_=wn[96:128, :, :].rearrange("p t n -> p n t"),
        )
        nc.vector.quantize_mx(out=gc[:].bitcast(FP8X4), scales=gs[:], in_=gin[:])
        nc.vector.quantize_mx(out=wgc[:].bitcast(FP8X4), scales=wgs[:], in_=wgin[:])
        nc.tensor.matmul_mx(
            out=cps[:, 0:128],
            lhsT=gc[:].bitcast(FP8X4),
            lhsT_scale=gs[:],
            rhs=wgc[:].bitcast(FP8X4),
            rhs_scale=wgs[:],
            start=True,
            stop=True,
        )
        multiply(0, 0)
        quantise(1)
        nc.vector.tensor_tensor(out=bias[:], in0=cps[:, 0:128], in1=bsb[:], op=ADD)
        multiply(0, 1)
        evacuate(2)

        for g in range(1, NG):
            if g + 2 < NG:
                transposes(g + 2)
            if g >= 2:
                relu_scalar(g - 2, 0, V_RELU, 1024)
                if g - 2 >= 10:
                    store(slice(1024 * (g - 2), 1024 * (g - 1)))
                elif g % 2 == 1:
                    store(slice(1024 * (g - 3), 1024 * (g - 1)))
            if g + 2 < NG:
                evacuate(g + 2)
            add_bias(g - 1, 0)
            multiply(g, 0)
            add_bias(g - 1, 1)
            multiply(g, 1)
            if g + 1 < NG:
                quantise(g + 1)
            if g + 1 < NG:
                relu_vector(g - 1, 0, 0, V_RELU)
        last = NG - 1
        for s in range(2):
            relu_scalar(last - 1, s)
            store(out_cols(last - 1, s))
        add_bias(last, 0)
        relu_scalar(last, 0)
        store(out_cols(last, 0))
        add_bias(last, 1)
        relu_vector(last, 1)
        store(out_cols(last, 1))
